import numpy as np
import ml_dtypes


def mxq(x, axis, fmt="e4m3"):
    dtype, down = {"e4m3": (ml_dtypes.float8_e4m3fn, 7), "e5m2": (ml_dtypes.float8_e5m2, 14)}[fmt]
    v = np.moveaxis(np.asarray(x, np.float32).astype(ml_dtypes.bfloat16).astype(np.float64), axis, -1)
    blocks = v.reshape(v.shape[:-1] + (-1, 32))
    amax = np.abs(blocks).max(-1, keepdims=True)
    byte = np.maximum(np.where(amax > 0, np.frexp(amax)[1] - 1 + 127, 0) - down, 1)
    scale = np.exp2(byte - 127.0)
    codes = (blocks / scale).astype(np.float32).astype(dtype).astype(np.float64)
    return np.moveaxis((codes * scale).reshape(v.shape), -1, axis)


WIDE = False


def mx_kscale(k):
    if not WIDE:
        return np.ones(k)
    levels = np.array([10, -10, 5, -5, 0])
    a = np.random.permutation(np.resize(levels, k // 512 * 4)).reshape(k // 512, 4)
    idx = np.arange(k)
    return np.exp2(a[idx // 512, idx % 128 // 32])


BF16 = ml_dtypes.bfloat16


def bf(x):
    return np.asarray(x, np.float32).astype(BF16)


def f64(x):
    return np.asarray(x).astype(np.float64)


B, K, N = 8192, 512, 256
EPS = 1e-5
GELU_C = 0.7978845608


def setup_inputs():
    s = mx_kscale(K)
    return {"x": bf(np.random.standard_normal((B, K)) * s),
            "weight": bf(np.random.standard_normal((K, N)) * np.sqrt(2.0 / K) / s[:, None]),
            "bn_gamma": bf(np.random.uniform(0.5, 1.5, N)),
            "bn_beta": bf(np.random.standard_normal(N) * 0.1),
            "bn_mean": bf(np.random.standard_normal(N) * 0.1),
            "bn_var": bf(np.random.uniform(0.5, 1.5, N))}


def reference(x, weight, bn_gamma, bn_beta, bn_mean, bn_var):
    acc = mxq(f64(x), 1, "e4m3") @ mxq(f64(weight), 0, "e4m3")
    x_norm = (acc - f64(bn_mean)) / np.sqrt(f64(bn_var) + EPS)
    bn_out = f64(bn_gamma) * x_norm + f64(bn_beta)
    gelu = 0.5 * bn_out * (1.0 + np.tanh(GELU_C * (bn_out + 0.044715 * bn_out * bn_out * bn_out)))
    return np.maximum(gelu, 0.0)

@@ -1,0 +1,232 @@
+from contextlib import ExitStack
+
+import concourse.masks as masks
+import concourse.mybir as mybir
+
+F32 = mybir.dt.float32
+BF16 = mybir.dt.bfloat16
+U32 = mybir.dt.uint32
+U8 = mybir.dt.uint8
+FP8X4 = mybir.dt.float8_e4m3fn_x4
+ACT = mybir.ActivationFunctionType
+ALU = mybir.AluOpType
+
+P = 128
+B, K, N = 8192, 512, 256
+EPS = 1e-5
+FLOPS = 2 * B * K * N
+
+UNIT = 512
+J = UNIT // P
+NU = B // UNIT
+LA = 2
+LG = 2
+
+
+def tile_modelnew_t_kernel(tc, x, weight, bn_gamma, bn_beta, bn_mean, bn_var, out):
+    nc = tc.nc
+    with ExitStack() as ctx:
+        ctx.enter_context(tc.manual_schedule())
+        const = ctx.enter_context(tc.tile_pool(name="const", bufs=1))
+        xin = ctx.enter_context(tc.tile_pool(name="xin", bufs=1))
+        work = ctx.enter_context(tc.tile_pool(name="work", bufs=3))
+        gpool = ctx.enter_context(tc.tile_pool(name="gpool", bufs=6))
+        opool = ctx.enter_context(tc.tile_pool(name="opool", bufs=1))
+        psum = ctx.enter_context(tc.psum_pool(name="psum", bufs=1))
+
+        prm_rows = const.tile([8, P], BF16)
+        for v, vec in enumerate((bn_gamma, bn_beta, bn_mean, bn_var)):
+            nc.scalar.dma_start(
+                out=prm_rows[2 * v : 2 * v + 2, :], in_=vec.rearrange("(h n) -> h n", h=2)
+            )
+        x_sb = []
+        w_raw = const.tile([P, 2, 2 * N], BF16)
+        for c in range(NU):
+            xt_c = xin.tile([P, J * K], BF16, name="x%d" % c)
+            nc.sync.dma_start(
+                out=xt_c[:],
+                in_=x[c * UNIT : (c + 1) * UNIT, :].rearrange("(p j) k -> p (j k)", j=J),
+            )
+            x_sb.append(xt_c)
+            if c == 0:
+                nc.sync.dma_start(
+                    out=w_raw[:], in_=weight.rearrange("(u p e) n -> p u (e n)", u=2, e=2)
+                )
+
+        warm = const.tile([P, 1], F32)
+        nc.vector.memset(warm[:], 0.0)
+        warm2 = const.tile([P, 1], F32)
+        nc.scalar.activation(out=warm2[:], in_=warm[:], func=ACT.Gelu_apprx_tanh)
+        ident = const.tile([P, P], F32)
+        masks.make_identity(nc, ident[:])
+        prm_f = const.tile([P, P], F32)
+        nc.vector.memset(prm_f[:], 0.0)
+        mhalf = const.tile([P, 2], F32)
+        nc.vector.memset(mhalf[:], -0.5)
+
+        w_grp = const.tile([P, N, 2, 2], BF16, align_bytes=64)
+        w_codes = const.tile([P, N], U32, align_bytes=64)
+        w_scales = const.tile([P, N], U8, align_bytes=64)
+        bn_s = const.tile([P, 2], F32)
+        bn_b = const.tile([P, 2], F32)
+
+        def prep_weight():
+            nc.vector.tensor_copy(
+                out=w_grp[:], in_=w_raw[:].rearrange("p u (e n) -> p n u e", e=2)
+            )
+            nc.vector.quantize_mx(
+                out=w_codes[:].bitcast(FP8X4),
+                scales=w_scales[:],
+                in_=w_grp[:].rearrange("p n u e -> p (n u e)"),
+            )
+
+        p_t = psum.tile([P, P], F32, tag="ot", bufs=3)
+        prm = const.tile([P, 8], F32)
+        veps = const.tile([P, 2], F32)
+        rstd = const.tile([P, 2], F32)
+        ms = const.tile([P, 2], F32)
+
+        def prep_bn_1():
+            nc.vector.tensor_copy(out=prm_f[0:8, :], in_=prm_rows[:])
+            nc.tensor.transpose(p_t[:], prm_f[:], ident[:])
+
+        def prep_bn_2():
+            nc.vector.tensor_copy(out=prm[:], in_=p_t[:, 0:8])
+            nc.vector.tensor_scalar_add(out=veps[:], in0=prm[:, 6:8], scalar1=EPS)
+            nc.gpsimd.tensor_tensor(out=rstd[:], in0=veps[:], in1=mhalf[:], op=ALU.pow)
+
+        def prep_bn_3():
+            nc.vector.tensor_mul(out=bn_s[:], in0=prm[:, 0:2], in1=rstd[:])
+            nc.vector.tensor_mul(out=ms[:], in0=prm[:, 4:6], in1=bn_s[:])
+            nc.vector.tensor_sub(out=bn_b[:], in0=prm[:, 2:4], in1=ms[:])
+
+        xt = {}
+        grp = {}
+        xq = {}
+        acc = {}
+        gel = {}
+        ot = {}
+        o_sb = {}
+
+        def stage_a(i):
+            words = x_sb[i][:].bitcast(F32)
+            for hb in range(2):
+                t = psum.tile([P, 2, 2, P], F32, tag="xt", bufs=3, name="xt%d_%d" % (i, hb))
+                for jj in range(2):
+                    for u in range(2):
+                        col = (2 * hb + jj) * (K // 2) + u * P
+                        nc.tensor.transpose(t[:, jj, u, :], words[:, col : col + P], ident[:])
+                xt[(i, hb)] = t
+
+        def stage_b(i, hb, eng):
+            if hb == 0:
+                grp[i] = work.tile([P, 4 * UNIT], BF16, tag="grp", align_bytes=64, name="grp%d" % i)
+            dst = grp[i][:].bitcast(F32)[:, hb * UNIT : (hb + 1) * UNIT].rearrange(
+                "p (j r u) -> p j r u", j=2, u=2
+            )
+            src = xt[(i, hb)][:].rearrange("p j u r -> p j r u")
+            if eng == "V":
+                nc.vector.tensor_copy(out=dst, in_=src)
+            else:
+                nc.scalar.copy(out=dst, in_=src)
+
+        def stage_c(i):
+            codes = work.tile([P, UNIT], U32, tag="xq", align_bytes=64, name="xq%d" % i)
+            scales = work.tile([P, UNIT], U8, tag="xs", align_bytes=64, name="xs%d" % i)
+            nc.vector.quantize_mx(out=codes[:].bitcast(FP8X4), scales=scales[:], in_=grp[i][:])
+            xq[i] = (codes, scales)
+
+        def stage_d(i):
+            codes, scales = xq[i]
+            for h in range(2):
+                a = psum.tile([P, UNIT], F32, tag="acc", bufs=2, name="acc%d_%d" % (i, h))
+                nc.tensor.matmul_mx(
+                    out=a[:],
+                    lhsT=w_codes[:, h * P : (h + 1) * P].bitcast(FP8X4),
+                    lhsT_scale=w_scales[:, h * P : (h + 1) * P],
+                    rhs=codes[:].bitcast(FP8X4),
+                    rhs_scale=scales[:],
+                    start=True,
+                    stop=True,
+                )
+                acc[(i, h)] = a
+
+        def stage_e(i):
+            for h in range(2):
+                g = gpool.tile([P, UNIT], F32, tag="g", name="g%d_%d" % (i, h))
+                nc.scalar.activation(
+                    out=g[:],
+                    in_=acc[(i, h)][:],
+                    func=ACT.Gelu_apprx_tanh,
+                    bias=bn_b[:, h : h + 1],
+                    scale=bn_s[:, h : h + 1],
+                )
+                gel[(i, h)] = g
+
+        def stage_f(i):
+            for hb in range(2):
+                t = psum.tile([P, 2, N], F32, tag="ot", bufs=3, name="ot%d_%d" % (i, hb))
+                for jj in range(2):
+                    for h in range(2):
+                        col = (2 * hb + jj) * P
+                        nc.tensor.transpose(
+                            t[:, jj, h * P : (h + 1) * P], gel[(i, h)][:, col : col + P], ident[:]
+                        )
+                ot[(i, hb)] = t
+
+        def stage_g(i, hb, eng):
+            if i not in o_sb:
+                o_sb[i] = opool.tile([P, J * N], F32, name="o%d" % i)
+            dst = o_sb[i][:, hb * 2 * N : (hb + 1) * 2 * N]
+            src = ot[(i, hb)][:].rearrange("p j n -> p (j n)")
+            if eng == "V":
+                nc.vector.tensor_scalar(
+                    out=dst, in0=src, scalar1=0.0, scalar2=0.0, op0=ALU.max, op1=ALU.add
+                )
+            else:
+                nc.scalar.activation(out=dst, in_=src, func=ACT.Relu)
+
+        def stage_h(i):
+            nc.sync.dma_start(
+                out=out[i * UNIT : (i + 1) * UNIT, :].rearrange("(p j) n -> p (j n)", j=J),
+                in_=o_sb[i][:],
+            )
+
+        def b_engine(i, hb):
+            return "S" if (i < 3 and hb == 1) else "V"
+
+        def g_engine(i, hb):
+            if i >= NU - 3:
+                return "V"
+            if hb == 1:
+                return "S"
+            return "V" if i % 2 == 0 else "S"
+
+        def live(i):
+            return 0 <= i < NU
+
+        for p in range(-LA, NU + LG + 1):
+            if live(p + 1):
+                stage_c(p + 1)
+            if live(p):
+                stage_d(p)
+            if live(p + LA):
+                stage_a(p + LA)
+            if live(p - 1):
+                stage_f(p - 1)
+            if live(p - LG):
+                stage_g(p - LG, 1, g_engine(p - LG, 1))
+            if live(p):
+                stage_e(p)
+            if live(p - LG):
+                stage_g(p - LG, 0, g_engine(p - LG, 0))
+                stage_h(p - LG)
+            if live(p + LA):
+                stage_b(p + LA, 0, b_engine(p + LA, 0))
+                stage_b(p + LA, 1, b_engine(p + LA, 1))
+            if p == -LA:
+                prep_bn_1()
+                prep_weight()
+                prep_bn_2()
+            if p == -LA + 1:
+                prep_bn_3()

@@ -39,19 +39,25 @@ def tile_modelnew_t_kernel(tc, x, weight, bn_gamma, bn_beta, bn_mean, bn_var, ou
             nc.scalar.dma_start(
                 out=prm_rows[2 * v : 2 * v + 2, :], in_=vec.rearrange("(h n) -> h n", h=2)
             )
-        x_sb = []
+        x_words = {}
         w_raw = const.tile([P, 2, 2 * N], BF16)
         for c in range(NU):
-            xt_c = xin.tile([P, J * K], BF16, name="x%d" % c)
-            nc.sync.dma_start(
-                out=xt_c[:],
-                in_=x[c * UNIT : (c + 1) * UNIT, :].rearrange("(p j) k -> p (j k)", j=J),
-            )
-            x_sb.append(xt_c)
+            rows = x[c * UNIT : (c + 1) * UNIT, :].rearrange("(p j) k -> p j k", j=J)
             if c == 0:
+                for hb in range(2):
+                    half = xin.tile([P, 2, K], BF16, name="x0_%d" % hb)
+                    nc.sync.dma_start(out=half[:], in_=rows[:, 2 * hb : 2 * hb + 2, :])
+                    x_words[(c, hb)] = half[:].rearrange("p j k -> p (j k)").bitcast(F32)
                 nc.sync.dma_start(
                     out=w_raw[:], in_=weight.rearrange("(u p e) n -> p u (e n)", u=2, e=2)
                 )
+            else:
+                whole = xin.tile([P, J, K], BF16, name="x%d" % c)
+                nc.sync.dma_start(out=whole[:], in_=rows)
+                for hb in range(2):
+                    x_words[(c, hb)] = (
+                        whole[:, 2 * hb : 2 * hb + 2, :].rearrange("p j k -> p (j k)").bitcast(F32)
+                    )
 
         warm = const.tile([P, 1], F32)
         nc.vector.memset(warm[:], 0.0)
@@ -80,7 +86,7 @@ def tile_modelnew_t_kernel(tc, x, weight, bn_gamma, bn_beta, bn_mean, bn_var, ou
                 in_=w_grp[:].rearrange("p n u e -> p (n u e)"),
             )
 
-        p_t = psum.tile([P, P], F32, tag="ot", bufs=3)
+        p_t = psum.tile([P, P], F32, tag="ot", bufs=2)
         prm = const.tile([P, 8], F32)
         veps = const.tile([P, 2], F32)
         rstd = const.tile([P, 2], F32)
@@ -109,12 +115,12 @@ def tile_modelnew_t_kernel(tc, x, weight, bn_gamma, bn_beta, bn_mean, bn_var, ou
         o_sb = {}
 
         def stage_a(i):
-            words = x_sb[i][:].bitcast(F32)
             for hb in range(2):
+                words = x_words[(i, hb)]
                 t = psum.tile([P, 2, 2, P], F32, tag="xt", bufs=3, name="xt%d_%d" % (i, hb))
                 for jj in range(2):
                     for u in range(2):
-                        col = (2 * hb + jj) * (K // 2) + u * P
+                        col = jj * (K // 2) + u * P
                         nc.tensor.transpose(t[:, jj, u, :], words[:, col : col + P], ident[:])
                 xt[(i, hb)] = t
 
@@ -139,7 +145,7 @@ def tile_modelnew_t_kernel(tc, x, weight, bn_gamma, bn_beta, bn_mean, bn_var, ou
         def stage_d(i):
             codes, scales = xq[i]
             for h in range(2):
-                a = psum.tile([P, UNIT], F32, tag="acc", bufs=2, name="acc%d_%d" % (i, h))
+                a = psum.tile([P, UNIT], F32, tag="acc", bufs=3, name="acc%d_%d" % (i, h))
                 nc.tensor.matmul_mx(
                     out=a[:],
                     lhsT=w_codes[:, h * P : (h + 1) * P].bitcast(FP8X4),
@@ -165,7 +171,7 @@ def tile_modelnew_t_kernel(tc, x, weight, bn_gamma, bn_beta, bn_mean, bn_var, ou
 
         def stage_f(i):
             for hb in range(2):
-                t = psum.tile([P, 2, N], F32, tag="ot", bufs=3, name="ot%d_%d" % (i, hb))
+                t = psum.tile([P, 2, N], F32, tag="ot", bufs=2, name="ot%d_%d" % (i, hb))
                 for jj in range(2):
                     for h in range(2):
                         col = (2 * hb + jj) * P
@@ -175,9 +181,13 @@ def tile_modelnew_t_kernel(tc, x, weight, bn_gamma, bn_beta, bn_mean, bn_var, ou
                 ot[(i, hb)] = t
 
         def stage_g(i, hb, eng):
-            if i not in o_sb:
-                o_sb[i] = opool.tile([P, J * N], F32, name="o%d" % i)
-            dst = o_sb[i][:, hb * 2 * N : (hb + 1) * 2 * N]
+            if i == NU - 1:
+                o_sb[(i, hb)] = opool.tile([P, 2 * N], F32, name="o%d_%d" % (i, hb))
+                dst = o_sb[(i, hb)][:]
+            else:
+                if hb == 0:
+                    o_sb[i] = opool.tile([P, J * N], F32, name="o%d" % i)
+                dst = o_sb[i][:, hb * 2 * N : (hb + 1) * 2 * N]
             src = ot[(i, hb)][:].rearrange("p j n -> p (j n)")
             if eng == "V":
                 nc.vector.tensor_scalar(
@@ -187,20 +197,27 @@ def tile_modelnew_t_kernel(tc, x, weight, bn_gamma, bn_beta, bn_mean, bn_var, ou
                 nc.scalar.activation(out=dst, in_=src, func=ACT.Relu)
 
         def stage_h(i):
-            nc.sync.dma_start(
-                out=out[i * UNIT : (i + 1) * UNIT, :].rearrange("(p j) n -> p (j n)", j=J),
-                in_=o_sb[i][:],
-            )
+            rows = out[i * UNIT : (i + 1) * UNIT, :].rearrange("(p j) n -> p j n", j=J)
+            if i == NU - 1:
+                for hb in range(2):
+                    nc.sync.dma_start(
+                        out=rows[:, 2 * hb : 2 * hb + 2, :],
+                        in_=o_sb[(i, hb)][:].rearrange("p (j n) -> p j n", j=2),
+                    )
+            else:
+                nc.sync.dma_start(out=rows, in_=o_sb[i][:].rearrange("p (j n) -> p j n", j=J))
 
         def b_engine(i, hb):
             return "S" if (i < 3 and hb == 1) else "V"
 
         def g_engine(i, hb):
+            if i == NU - 1:
+                return "V" if hb == 0 else "S"
             if i >= NU - 3:
                 return "V"
             if hb == 1:
                 return "S"
-            return "V" if i % 2 == 0 else "S"
+            return "V" if i % 4 == 0 else "S"
 
         def live(i):
             return 0 <= i < NU
@@ -215,12 +232,11 @@ def tile_modelnew_t_kernel(tc, x, weight, bn_gamma, bn_beta, bn_mean, bn_var, ou
             if live(p - 1):
                 stage_f(p - 1)
             if live(p - LG):
+                stage_g(p - LG, 0, g_engine(p - LG, 0))
                 stage_g(p - LG, 1, g_engine(p - LG, 1))
+                stage_h(p - LG)
             if live(p):
                 stage_e(p)
-            if live(p - LG):
-                stage_g(p - LG, 0, g_engine(p - LG, 0))
-                stage_h(p - LG)
             if live(p + LA):
                 stage_b(p + LA, 0, b_engine(p + LA, 0))
                 stage_b(p + LA, 1, b_engine(p + LA, 1))

@@ -26,7 +26,6 @@ LG = 2
 def tile_modelnew_t_kernel(tc, x, weight, bn_gamma, bn_beta, bn_mean, bn_var, out):
     nc = tc.nc
     with ExitStack() as ctx:
-        ctx.enter_context(tc.manual_schedule())
         const = ctx.enter_context(tc.tile_pool(name="const", bufs=1))
         xin = ctx.enter_context(tc.tile_pool(name="xin", bufs=1))
         work = ctx.enter_context(tc.tile_pool(name="work", bufs=3))

from contextlib import ExitStack

import concourse.masks as masks
import concourse.mybir as mybir

F32 = mybir.dt.float32
BF16 = mybir.dt.bfloat16
U32 = mybir.dt.uint32
U8 = mybir.dt.uint8
FP8X4 = mybir.dt.float8_e4m3fn_x4
ACT = mybir.ActivationFunctionType
ALU = mybir.AluOpType

P = 128
B, K, N = 8192, 512, 256
EPS = 1e-5
FLOPS = 2 * B * K * N

UNIT = 512
J = UNIT // P
NU = B // UNIT
LA = 2
LG = 2


def tile_modelnew_t_kernel(tc, x, weight, bn_gamma, bn_beta, bn_mean, bn_var, out):
    nc = tc.nc
    with ExitStack() as ctx:
        const = ctx.enter_context(tc.tile_pool(name="const", bufs=1))
        xin = ctx.enter_context(tc.tile_pool(name="xin", bufs=1))
        work = ctx.enter_context(tc.tile_pool(name="work", bufs=3))
        gpool = ctx.enter_context(tc.tile_pool(name="gpool", bufs=6))
        opool = ctx.enter_context(tc.tile_pool(name="opool", bufs=1))
        psum = ctx.enter_context(tc.psum_pool(name="psum", bufs=1))

        prm_rows = const.tile([8, P], BF16)
        for v, vec in enumerate((bn_gamma, bn_beta, bn_mean, bn_var)):
            nc.scalar.dma_start(
                out=prm_rows[2 * v : 2 * v + 2, :], in_=vec.rearrange("(h n) -> h n", h=2)
            )
        x_words = {}
        w_raw = const.tile([P, 2, 2 * N], BF16)
        for c in range(NU):
            rows = x[c * UNIT : (c + 1) * UNIT, :].rearrange("(p j) k -> p j k", j=J)
            if c == 0:
                for hb in range(2):
                    half = xin.tile([P, 2, K], BF16, name="x0_%d" % hb)
                    nc.sync.dma_start(out=half[:], in_=rows[:, 2 * hb : 2 * hb + 2, :])
                    x_words[(c, hb)] = half[:].rearrange("p j k -> p (j k)").bitcast(F32)
                nc.sync.dma_start(
                    out=w_raw[:], in_=weight.rearrange("(u p e) n -> p u (e n)", u=2, e=2)
                )
            else:
                whole = xin.tile([P, J, K], BF16, name="x%d" % c)
                nc.sync.dma_start(out=whole[:], in_=rows)
                for hb in range(2):
                    x_words[(c, hb)] = (
                        whole[:, 2 * hb : 2 * hb + 2, :].rearrange("p j k -> p (j k)").bitcast(F32)
                    )

        warm = const.tile([P, 1], F32)
        nc.vector.memset(warm[:], 0.0)
        warm2 = const.tile([P, 1], F32)
        nc.scalar.activation(out=warm2[:], in_=warm[:], func=ACT.Gelu_apprx_tanh)
        ident = const.tile([P, P], F32)
        masks.make_identity(nc, ident[:])
        prm_f = const.tile([P, P], F32)
        nc.vector.memset(prm_f[:], 0.0)
        mhalf = const.tile([P, 2], F32)
        nc.vector.memset(mhalf[:], -0.5)

        w_grp = const.tile([P, N, 2, 2], BF16, align_bytes=64)
        w_codes = const.tile([P, N], U32, align_bytes=64)
        w_scales = const.tile([P, N], U8, align_bytes=64)
        bn_s = const.tile([P, 2], F32)
        bn_b = const.tile([P, 2], F32)

        def prep_weight():
            nc.vector.tensor_copy(
                out=w_grp[:], in_=w_raw[:].rearrange("p u (e n) -> p n u e", e=2)
            )
            nc.vector.quantize_mx(
                out=w_codes[:].bitcast(FP8X4),
                scales=w_scales[:],
                in_=w_grp[:].rearrange("p n u e -> p (n u e)"),
            )

        p_t = psum.tile([P, P], F32, tag="ot", bufs=2)
        prm = const.tile([P, 8], F32)
        veps = const.tile([P, 2], F32)
        rstd = const.tile([P, 2], F32)
        ms = const.tile([P, 2], F32)

        def prep_bn_1():
            nc.vector.tensor_copy(out=prm_f[0:8, :], in_=prm_rows[:])
            nc.tensor.transpose(p_t[:], prm_f[:], ident[:])

        def prep_bn_2():
            nc.vector.tensor_copy(out=prm[:], in_=p_t[:, 0:8])
            nc.vector.tensor_scalar_add(out=veps[:], in0=prm[:, 6:8], scalar1=EPS)
            nc.gpsimd.tensor_tensor(out=rstd[:], in0=veps[:], in1=mhalf[:], op=ALU.pow)

        def prep_bn_3():
            nc.vector.tensor_mul(out=bn_s[:], in0=prm[:, 0:2], in1=rstd[:])
            nc.vector.tensor_mul(out=ms[:], in0=prm[:, 4:6], in1=bn_s[:])
            nc.vector.tensor_sub(out=bn_b[:], in0=prm[:, 2:4], in1=ms[:])

        xt = {}
        grp = {}
        xq = {}
        acc = {}
        gel = {}
        ot = {}
        o_sb = {}

        def stage_a(i):
            for hb in range(2):
                words = x_words[(i, hb)]
                t = psum.tile([P, 2, 2, P], F32, tag="xt", bufs=3, name="xt%d_%d" % (i, hb))
                for jj in range(2):
                    for u in range(2):
                        col = jj * (K // 2) + u * P
                        nc.tensor.transpose(t[:, jj, u, :], words[:, col : col + P], ident[:])
                xt[(i, hb)] = t

        def stage_b(i, hb, eng):
            if hb == 0:
                grp[i] = work.tile([P, 4 * UNIT], BF16, tag="grp", align_bytes=64, name="grp%d" % i)
            dst = grp[i][:].bitcast(F32)[:, hb * UNIT : (hb + 1) * UNIT].rearrange(
                "p (j r u) -> p j r u", j=2, u=2
            )
            src = xt[(i, hb)][:].rearrange("p j u r -> p j r u")
            if eng == "V":
                nc.vector.tensor_copy(out=dst, in_=src)
            else:
                nc.scalar.copy(out=dst, in_=src)

        def stage_c(i):
            codes = work.tile([P, UNIT], U32, tag="xq", align_bytes=64, name="xq%d" % i)
            scales = work.tile([P, UNIT], U8, tag="xs", align_bytes=64, name="xs%d" % i)
            nc.vector.quantize_mx(out=codes[:].bitcast(FP8X4), scales=scales[:], in_=grp[i][:])
            xq[i] = (codes, scales)

        def stage_d(i):
            codes, scales = xq[i]
            for h in range(2):
                a = psum.tile([P, UNIT], F32, tag="acc", bufs=3, name="acc%d_%d" % (i, h))
                nc.tensor.matmul_mx(
                    out=a[:],
                    lhsT=w_codes[:, h * P : (h + 1) * P].bitcast(FP8X4),
                    lhsT_scale=w_scales[:, h * P : (h + 1) * P],
                    rhs=codes[:].bitcast(FP8X4),
                    rhs_scale=scales[:],
                    start=True,
                    stop=True,
                )
                acc[(i, h)] = a

        def stage_e(i):
            for h in range(2):
                g = gpool.tile([P, UNIT], F32, tag="g", name="g%d_%d" % (i, h))
                nc.scalar.activation(
                    out=g[:],
                    in_=acc[(i, h)][:],
                    func=ACT.Gelu_apprx_tanh,
                    bias=bn_b[:, h : h + 1],
                    scale=bn_s[:, h : h + 1],
                )
                gel[(i, h)] = g

        def stage_f(i):
            for hb in range(2):
                t = psum.tile([P, 2, N], F32, tag="ot", bufs=2, name="ot%d_%d" % (i, hb))
                for jj in range(2):
                    for h in range(2):
                        col = (2 * hb + jj) * P
                        nc.tensor.transpose(
                            t[:, jj, h * P : (h + 1) * P], gel[(i, h)][:, col : col + P], ident[:]
                        )
                ot[(i, hb)] = t

        def stage_g(i, hb, eng):
            if i == NU - 1:
                o_sb[(i, hb)] = opool.tile([P, 2 * N], F32, name="o%d_%d" % (i, hb))
                dst = o_sb[(i, hb)][:]
            else:
                if hb == 0:
                    o_sb[i] = opool.tile([P, J * N], F32, name="o%d" % i)
                dst = o_sb[i][:, hb * 2 * N : (hb + 1) * 2 * N]
            src = ot[(i, hb)][:].rearrange("p j n -> p (j n)")
            if eng == "V":
                nc.vector.tensor_scalar(
                    out=dst, in0=src, scalar1=0.0, scalar2=0.0, op0=ALU.max, op1=ALU.add
                )
            else:
                nc.scalar.activation(out=dst, in_=src, func=ACT.Relu)

        def stage_h(i):
            rows = out[i * UNIT : (i + 1) * UNIT, :].rearrange("(p j) n -> p j n", j=J)
            if i == NU - 1:
                for hb in range(2):
                    nc.sync.dma_start(
                        out=rows[:, 2 * hb : 2 * hb + 2, :],
                        in_=o_sb[(i, hb)][:].rearrange("p (j n) -> p j n", j=2),
                    )
            else:
                nc.sync.dma_start(out=rows, in_=o_sb[i][:].rearrange("p (j n) -> p j n", j=J))

        def b_engine(i, hb):
            return "S" if (i < 3 and hb == 1) else "V"

        def g_engine(i, hb):
            if i == NU - 1:
                return "V" if hb == 0 else "S"
            if i >= NU - 3:
                return "V"
            if hb == 1:
                return "S"
            return "V" if i % 4 == 0 else "S"

        def live(i):
            return 0 <= i < NU

        for p in range(-LA, NU + LG + 1):
            if live(p + 1):
                stage_c(p + 1)
            if live(p):
                stage_d(p)
            if live(p + LA):
                stage_a(p + LA)
            if live(p - 1):
                stage_f(p - 1)
            if live(p - LG):
                stage_g(p - LG, 0, g_engine(p - LG, 0))
                stage_g(p - LG, 1, g_engine(p - LG, 1))
                stage_h(p - LG)
            if live(p):
                stage_e(p)
            if live(p + LA):
                stage_b(p + LA, 0, b_engine(p + LA, 0))
                stage_b(p + LA, 1, b_engine(p + LA, 1))
            if p == -LA:
                prep_bn_1()
                prep_weight()
                prep_bn_2()
            if p == -LA + 1:
                prep_bn_3()
